import numpy as np
import ml_dtypes


def mxq(x, axis, fmt="e4m3"):
    dtype, down = {"e4m3": (ml_dtypes.float8_e4m3fn, 7), "e5m2": (ml_dtypes.float8_e5m2, 14)}[fmt]
    v = np.moveaxis(np.asarray(x, np.float32).astype(ml_dtypes.bfloat16).astype(np.float64), axis, -1)
    blocks = v.reshape(v.shape[:-1] + (-1, 32))
    amax = np.abs(blocks).max(-1, keepdims=True)
    byte = np.maximum(np.where(amax > 0, np.frexp(amax)[1] - 1 + 127, 0) - down, 1)
    scale = np.exp2(byte - 127.0)
    codes = (blocks / scale).astype(np.float32).astype(dtype).astype(np.float64)
    return np.moveaxis((codes * scale).reshape(v.shape), -1, axis)


WIDE = False


def mx_kscale(k):
    if not WIDE:
        return np.ones(k)
    levels = np.array([10, -10, 5, -5, 0])
    if k % 512:
        return np.exp2(np.random.permutation(np.resize(levels, k // 32))).repeat(32)
    a = np.empty((k // 512, 16))
    for p in range(k // 512):
        a[p, :8] = np.random.permutation(np.resize(levels, 8))
        for g in range(8):
            far = levels[np.abs(levels - a[p, g]) >= 10]
            a[p, g + 8] = far[np.random.randint(len(far))]
    return np.exp2(a.ravel()).repeat(32)


BF16 = ml_dtypes.bfloat16


def bf(x):
    return np.asarray(x, np.float32).astype(BF16)


def f64(x):
    return np.asarray(x).astype(np.float64)


B, S, IN, OUT, SP = 4, 2048, 512, 384, 128


def setup_inputs():
    s = mx_kscale(IN)
    return {"x": bf(np.random.standard_normal((B, S, IN)) * s),
            "weights": bf(np.random.standard_normal((OUT, IN)) / np.sqrt(IN) / s[None, :])}


def reference(x, weights):
    x = f64(x)
    weights = f64(weights)
    size_out = x.shape[:-1] + (OUT,)
    xf = x.reshape(-1, x.shape[-1])
    xq = mxq(xf, 1, "e4m3")
    w_sparse = weights[:SP, :]
    w_dense = weights[SP:, :]
    out_sparse = xq @ mxq(w_sparse, 1, "e4m3").T
    out_dense = xq @ mxq(w_dense, 1, "e4m3").T
    out = np.concatenate([out_sparse, out_dense], axis=1)
    return out.reshape(size_out)

@@ -1,0 +1,156 @@
+from contextlib import ExitStack
+
+import concourse.mybir as mybir
+from concourse.masks import make_identity
+
+FP8X4 = mybir.dt.float8_e4m3fn_x4
+BF16 = mybir.dt.bfloat16
+F32 = mybir.dt.float32
+U32 = mybir.dt.uint32
+U8 = mybir.dt.uint8
+
+P = 128
+TOKENS = 8192
+K = 512
+KW = K // 2
+OUT = 384
+SPARSE = 128
+T = TOKENS // P
+GROUP = 4
+GROUPS = T // GROUP
+LOAD_CHUNKS = [4, 4, 8, 16, 32]
+STORE_CHUNKS = [8, 8, 8, 8, 8, 8, 8, 4, 4]
+
+FLOPS = 2 * TOKENS * K * OUT
+
+
+def tile_myinterleavedmodule_t_kernel(tc, x, weights, out):
+    nc = tc.nc
+    x_rows = x.flatten_outer_dims().rearrange("(p t) k -> p (t k)", t=T)
+    out_rows = out.flatten_outer_dims().rearrange("(p t) n -> p (t n)", t=T)
+    w_rows = weights.rearrange("(j p) k -> p j k", p=P)
+
+    with ExitStack() as ctx:
+        keep = ctx.enter_context(tc.tile_pool(name="keep", bufs=1))
+        work = ctx.enter_context(tc.tile_pool(name="work", bufs=3))
+        psum_t = ctx.enter_context(tc.psum_pool(name="psum_t", bufs=4))
+        psum_o = ctx.enter_context(tc.psum_pool(name="psum_o", bufs=4))
+        ctx.enter_context(tc.manual_schedule())
+
+        w_sb = keep.tile([P, 3 * K], BF16, name="w_sb")
+        nc.sync.dma_start(out=w_sb[:].rearrange("p (j k) -> p j k", j=3), in_=w_rows)
+        x_of_tile = []
+        t0 = 0
+        for c, n in enumerate(LOAD_CHUNKS):
+            x_sb = keep.tile([P, n * K], BF16, name="x_sb%d" % c)
+            nc.sync.dma_start(out=x_sb[:], in_=x_rows[:, t0 * K : (t0 + n) * K])
+            for i in range(n):
+                x_of_tile.append((x_sb[:].bitcast(F32), i))
+            t0 += n
+
+        out_of_tile = []
+        store_after = {}
+        t0 = 0
+        for c, n in enumerate(STORE_CHUNKS):
+            o_sb = keep.tile([P, n * OUT], F32, name="o_sb%d" % c)
+            for i in range(n):
+                out_of_tile.append((o_sb, i))
+            store_after[t0 + n - 1] = (o_sb, t0, n)
+            t0 += n
+
+        ident = keep.tile([P, P], F32, name="ident")
+        make_identity(nc, ident[:])
+
+        w_words = w_sb[:].bitcast(F32)
+        w_grouped = keep.tile([P, OUT * 4], BF16, name="w_grouped", align_bytes=64)
+        w_codes = keep.tile([P, OUT], U32, name="w_codes", align_bytes=64)
+        w_scales = keep.tile([P, OUT], U8, name="w_scales", align_bytes=64)
+        w_gw = w_grouped[:].bitcast(F32)
+        for b, tiles in enumerate([[0, 1], [2]]):
+            bank = psum_t.tile([P, 2, 2, P], F32, name="bank")
+            for i, j in enumerate(tiles):
+                for u in range(2):
+                    nc.tensor.transpose(
+                        bank[:, i, u, :], w_words[:, j * KW + u : (j + 1) * KW : 2], ident[:]
+                    )
+            n = len(tiles)
+            nc.vector.tensor_copy(
+                out=w_gw[:, 512 * b : 512 * b + 256 * n].rearrange(
+                    "p (i r u) -> p i r u", i=n, u=2
+                ),
+                in_=bank[:, 0:n, :, :].rearrange("p i u r -> p i r u"),
+            )
+        for lo, hi in [(0, SPARSE), (SPARSE, OUT)]:
+            nc.vector.quantize_mx(
+                out=w_codes[:, lo:hi].bitcast(FP8X4),
+                scales=w_scales[:, lo:hi],
+                in_=w_grouped[:, 4 * lo : 4 * hi],
+            )
+
+        banks = {}
+        grouped = {}
+        packed = {}
+
+        def transposes(g):
+            banks[g] = []
+            for b in range(GROUP // 2):
+                bank = psum_t.tile([P, 2, 2, P], F32, name="bank")
+                for i in range(2):
+                    words, idx = x_of_tile[g * GROUP + 2 * b + i]
+                    for u in range(2):
+                        lo = idx * KW
+                        nc.tensor.transpose(
+                            bank[:, i, u, :], words[:, lo + u : lo + KW : 2], ident[:]
+                        )
+                banks[g].append(bank)
+
+        def regroup(g):
+            grp = work.tile([P, GROUP * P * 4], BF16, name="grp", align_bytes=64)
+            gw = grp[:].bitcast(F32)
+            for b, bank in enumerate(banks[g]):
+                nc.vector.tensor_copy(
+                    out=gw[:, 512 * b : 512 * (b + 1)].rearrange("p (i r u) -> p i r u", i=2, u=2),
+                    in_=bank[:].rearrange("p i u r -> p i r u"),
+                )
+            grouped[g] = grp
+
+        def quantise(g):
+            codes = work.tile([P, GROUP * P], U32, name="codes", align_bytes=64)
+            scales = work.tile([P, GROUP * P], U8, name="scales", align_bytes=64)
+            nc.vector.quantize_mx(
+                out=codes[:].bitcast(FP8X4), scales=scales[:], in_=grouped[g][:]
+            )
+            packed[g] = (codes, scales)
+
+        def multiply(g):
+            codes, scales = packed[g]
+            for i in range(GROUP):
+                t = g * GROUP + i
+                cols = slice(i * P, (i + 1) * P)
+                acc = psum_o.tile([P, OUT], F32, name="acc")
+                for lo, hi in [(0, SPARSE), (SPARSE, OUT)]:
+                    nc.tensor.matmul_mx(
+                        out=acc[:, lo:hi],
+                        lhsT=codes[:, cols].bitcast(FP8X4),
+                        lhsT_scale=scales[:, cols],
+                        rhs=w_codes[:, lo:hi].bitcast(FP8X4),
+                        rhs_scale=w_scales[:, lo:hi],
+                        start=True,
+                        stop=True,
+                    )
+                o_sb, idx = out_of_tile[t]
+                nc.scalar.copy(out=o_sb[:, idx * OUT : (idx + 1) * OUT], in_=acc[:])
+                if t in store_after:
+                    o_sb, first, n = store_after[t]
+                    nc.sync.dma_start(
+                        out=out_rows[:, first * OUT : (first + n) * OUT], in_=o_sb[:]
+                    )
+
+        for s in range(GROUPS + 2):
+            if s < GROUPS:
+                transposes(s)
+                regroup(s)
+            if 1 <= s <= GROUPS:
+                quantise(s - 1)
+            if s >= 2:
+                multiply(s - 2)

@@ -37,12 +37,12 @@ def tile_myinterleavedmodule_t_kernel(tc, x, weights, out):
         psum_o = ctx.enter_context(tc.psum_pool(name="psum_o", bufs=4))
         ctx.enter_context(tc.manual_schedule())
 
-        w_sb = keep.tile([P, 3 * K], BF16, name="w_sb")
+        w_sb = keep.tile([P, 3 * K], BF16, name="w_sb", align_bytes=256)
         nc.sync.dma_start(out=w_sb[:].rearrange("p (j k) -> p j k", j=3), in_=w_rows)
         x_of_tile = []
         t0 = 0
         for c, n in enumerate(LOAD_CHUNKS):
-            x_sb = keep.tile([P, n * K], BF16, name="x_sb%d" % c)
+            x_sb = keep.tile([P, n * K], BF16, name="x_sb%d" % c, align_bytes=256)
             nc.sync.dma_start(out=x_sb[:], in_=x_rows[:, t0 * K : (t0 + n) * K])
             for i in range(n):
                 x_of_tile.append((x_sb[:].bitcast(F32), i))
@@ -52,7 +52,7 @@ def tile_myinterleavedmodule_t_kernel(tc, x, weights, out):
         store_after = {}
         t0 = 0
         for c, n in enumerate(STORE_CHUNKS):
-            o_sb = keep.tile([P, n * OUT], F32, name="o_sb%d" % c)
+            o_sb = keep.tile([P, n * OUT], F32, name="o_sb%d" % c, align_bytes=256)
             for i in range(n):
                 out_of_tile.append((o_sb, i))
             store_after[t0 + n - 1] = (o_sb, t0, n)

@@ -18,8 +18,9 @@ SPARSE = 128
 T = TOKENS // P
 GROUP = 4
 GROUPS = T // GROUP
-LOAD_CHUNKS = [4, 4, 8, 16, 32]
-STORE_CHUNKS = [8, 8, 8, 8, 8, 8, 8, 4, 4]
+LOAD_CHUNKS = [4, 8, 12, 20, 20]
+STORE_CHUNKS = [8, 8, 8, 8, 8, 8, 8, 4, 2, 2]
+SHARED_GROUPS = 2
 
 FLOPS = 2 * TOKENS * K * OUT
 
@@ -139,7 +140,11 @@ def tile_myinterleavedmodule_t_kernel(tc, x, weights, out):
                         stop=True,
                     )
                 o_sb, idx = out_of_tile[t]
-                nc.scalar.copy(out=o_sb[:, idx * OUT : (idx + 1) * OUT], in_=acc[:])
+                dst = o_sb[:, idx * OUT : (idx + 1) * OUT]
+                if g >= GROUPS - SHARED_GROUPS and i % 2 == 1:
+                    nc.vector.tensor_copy(out=dst, in_=acc[:])
+                else:
+                    nc.scalar.copy(out=dst, in_=acc[:])
                 if t in store_after:
                     o_sb, first, n = store_after[t]
                     nc.sync.dma_start(

@@ -22,6 +22,8 @@ LOAD_CHUNKS = [4, 8, 12, 20, 20]
 STORE_CHUNKS = [8, 8, 8, 8, 8, 8, 8, 4, 2, 2]
 SHARED_GROUPS = 2
 
+SPLIT_FROM = 4
+
 FLOPS = 2 * TOKENS * K * OUT
 
 
@@ -29,7 +31,7 @@ def tile_myinterleavedmodule_t_kernel(tc, x, weights, out):
     nc = tc.nc
     x_rows = x.flatten_outer_dims().rearrange("(p t) k -> p (t k)", t=T)
     out_rows = out.flatten_outer_dims().rearrange("(p t) n -> p (t n)", t=T)
-    w_rows = weights.rearrange("(j p) k -> p j k", p=P)
+    w_rows = weights.rearrange("(p j) k -> p (j k)", p=P)
 
     with ExitStack() as ctx:
         keep = ctx.enter_context(tc.tile_pool(name="keep", bufs=1))
@@ -39,7 +41,7 @@ def tile_myinterleavedmodule_t_kernel(tc, x, weights, out):
         ctx.enter_context(tc.manual_schedule())
 
         w_sb = keep.tile([P, 3 * K], BF16, name="w_sb", align_bytes=256)
-        nc.sync.dma_start(out=w_sb[:].rearrange("p (j k) -> p j k", j=3), in_=w_rows)
+        nc.sync.dma_start(out=w_sb[:], in_=w_rows)
         x_of_tile = []
         t0 = 0
         for c, n in enumerate(LOAD_CHUNKS):
@@ -66,7 +68,7 @@ def tile_myinterleavedmodule_t_kernel(tc, x, weights, out):
         w_grouped = keep.tile([P, OUT * 4], BF16, name="w_grouped", align_bytes=64)
         w_codes = keep.tile([P, OUT], U32, name="w_codes", align_bytes=64)
         w_scales = keep.tile([P, OUT], U8, name="w_scales", align_bytes=64)
-        w_gw = w_grouped[:].bitcast(F32)
+        w_gw = w_grouped[:].bitcast(F32).rearrange("p (r j u) -> p j r u", j=3, u=2)
         for b, tiles in enumerate([[0, 1], [2]]):
             bank = psum_t.tile([P, 2, 2, P], F32, name="bank")
             for i, j in enumerate(tiles):
@@ -75,34 +77,50 @@ def tile_myinterleavedmodule_t_kernel(tc, x, weights, out):
                         bank[:, i, u, :], w_words[:, j * KW + u : (j + 1) * KW : 2], ident[:]
                     )
             n = len(tiles)
-            nc.vector.tensor_copy(
-                out=w_gw[:, 512 * b : 512 * b + 256 * n].rearrange(
-                    "p (i r u) -> p i r u", i=n, u=2
-                ),
+            nc.scalar.copy(
+                out=w_gw[:, tiles[0] : tiles[0] + n],
                 in_=bank[:, 0:n, :, :].rearrange("p i u r -> p i r u"),
             )
-        for lo, hi in [(0, SPARSE), (SPARSE, OUT)]:
-            nc.vector.quantize_mx(
-                out=w_codes[:, lo:hi].bitcast(FP8X4),
-                scales=w_scales[:, lo:hi],
-                in_=w_grouped[:, 4 * lo : 4 * hi],
-            )
+
+        def quantise_weights():
+            for lo, hi in [(0, SPARSE), (SPARSE, OUT)]:
+                nc.vector.quantize_mx(
+                    out=w_codes[:, lo:hi].bitcast(FP8X4),
+                    scales=w_scales[:, lo:hi],
+                    in_=w_grouped[:, 4 * lo : 4 * hi],
+                )
 
         banks = {}
         grouped = {}
         packed = {}
+
+        split = {}
+
+        def split_words(g):
+            for i, copy in [(1, nc.scalar.copy), (3, nc.vector.tensor_copy)]:
+                t = g * GROUP + i
+                words, idx = x_of_tile[t]
+                dst = work.tile([P, 2, P], F32, name="split%d" % i)
+                copy(
+                    out=dst[:],
+                    in_=words[:, idx * KW : (idx + 1) * KW].rearrange("p (w u) -> p u w", u=2),
+                )
+                split[t] = dst
 
         def transposes(g):
             banks[g] = []
             for b in range(GROUP // 2):
                 bank = psum_t.tile([P, 2, 2, P], F32, name="bank")
                 for i in range(2):
-                    words, idx = x_of_tile[g * GROUP + 2 * b + i]
+                    t = g * GROUP + 2 * b + i
+                    words, idx = x_of_tile[t]
+                    lo = idx * KW
                     for u in range(2):
-                        lo = idx * KW
-                        nc.tensor.transpose(
-                            bank[:, i, u, :], words[:, lo + u : lo + KW : 2], ident[:]
-                        )
+                        if t in split:
+                            source = split[t][:, u, :]
+                        else:
+                            source = words[:, lo + u : lo + KW : 2]
+                        nc.tensor.transpose(bank[:, i, u, :], source, ident[:])
                 banks[g].append(bank)
 
         def regroup(g):
@@ -152,9 +170,13 @@ def tile_myinterleavedmodule_t_kernel(tc, x, weights, out):
                     )
 
         for s in range(GROUPS + 2):
+            if SPLIT_FROM <= s + 1 < GROUPS:
+                split_words(s + 1)
             if s < GROUPS:
                 transposes(s)
                 regroup(s)
+            if s == 0:
+                quantise_weights()
             if 1 <= s <= GROUPS:
                 quantise(s - 1)
             if s >= 2:

from contextlib import ExitStack

import concourse.mybir as mybir
from concourse.masks import make_identity

FP8X4 = mybir.dt.float8_e4m3fn_x4
BF16 = mybir.dt.bfloat16
F32 = mybir.dt.float32
U32 = mybir.dt.uint32
U8 = mybir.dt.uint8

P = 128
TOKENS = 8192
K = 512
KW = K // 2
OUT = 384
SPARSE = 128
T = TOKENS // P
GROUP = 4
GROUPS = T // GROUP
LOAD_CHUNKS = [4, 8, 12, 20, 20]
STORE_CHUNKS = [8, 8, 8, 8, 8, 8, 8, 4, 2, 2]
SHARED_GROUPS = 2

SPLIT_FROM = 4

FLOPS = 2 * TOKENS * K * OUT


def tile_myinterleavedmodule_t_kernel(tc, x, weights, out):
    nc = tc.nc
    x_rows = x.flatten_outer_dims().rearrange("(p t) k -> p (t k)", t=T)
    out_rows = out.flatten_outer_dims().rearrange("(p t) n -> p (t n)", t=T)
    w_rows = weights.rearrange("(p j) k -> p (j k)", p=P)

    with ExitStack() as ctx:
        keep = ctx.enter_context(tc.tile_pool(name="keep", bufs=1))
        work = ctx.enter_context(tc.tile_pool(name="work", bufs=3))
        psum_t = ctx.enter_context(tc.psum_pool(name="psum_t", bufs=4))
        psum_o = ctx.enter_context(tc.psum_pool(name="psum_o", bufs=4))
        ctx.enter_context(tc.manual_schedule())

        w_sb = keep.tile([P, 3 * K], BF16, name="w_sb", align_bytes=256)
        nc.sync.dma_start(out=w_sb[:], in_=w_rows)
        x_of_tile = []
        t0 = 0
        for c, n in enumerate(LOAD_CHUNKS):
            x_sb = keep.tile([P, n * K], BF16, name="x_sb%d" % c, align_bytes=256)
            nc.sync.dma_start(out=x_sb[:], in_=x_rows[:, t0 * K : (t0 + n) * K])
            for i in range(n):
                x_of_tile.append((x_sb[:].bitcast(F32), i))
            t0 += n

        out_of_tile = []
        store_after = {}
        t0 = 0
        for c, n in enumerate(STORE_CHUNKS):
            o_sb = keep.tile([P, n * OUT], F32, name="o_sb%d" % c, align_bytes=256)
            for i in range(n):
                out_of_tile.append((o_sb, i))
            store_after[t0 + n - 1] = (o_sb, t0, n)
            t0 += n

        ident = keep.tile([P, P], F32, name="ident")
        make_identity(nc, ident[:])

        w_words = w_sb[:].bitcast(F32)
        w_grouped = keep.tile([P, OUT * 4], BF16, name="w_grouped", align_bytes=64)
        w_codes = keep.tile([P, OUT], U32, name="w_codes", align_bytes=64)
        w_scales = keep.tile([P, OUT], U8, name="w_scales", align_bytes=64)
        w_gw = w_grouped[:].bitcast(F32).rearrange("p (r j u) -> p j r u", j=3, u=2)
        for b, tiles in enumerate([[0, 1], [2]]):
            bank = psum_t.tile([P, 2, 2, P], F32, name="bank")
            for i, j in enumerate(tiles):
                for u in range(2):
                    nc.tensor.transpose(
                        bank[:, i, u, :], w_words[:, j * KW + u : (j + 1) * KW : 2], ident[:]
                    )
            n = len(tiles)
            nc.scalar.copy(
                out=w_gw[:, tiles[0] : tiles[0] + n],
                in_=bank[:, 0:n, :, :].rearrange("p i u r -> p i r u"),
            )

        def quantise_weights():
            for lo, hi in [(0, SPARSE), (SPARSE, OUT)]:
                nc.vector.quantize_mx(
                    out=w_codes[:, lo:hi].bitcast(FP8X4),
                    scales=w_scales[:, lo:hi],
                    in_=w_grouped[:, 4 * lo : 4 * hi],
                )

        banks = {}
        grouped = {}
        packed = {}

        split = {}

        def split_words(g):
            for i, copy in [(1, nc.scalar.copy), (3, nc.vector.tensor_copy)]:
                t = g * GROUP + i
                words, idx = x_of_tile[t]
                dst = work.tile([P, 2, P], F32, name="split%d" % i)
                copy(
                    out=dst[:],
                    in_=words[:, idx * KW : (idx + 1) * KW].rearrange("p (w u) -> p u w", u=2),
                )
                split[t] = dst

        def transposes(g):
            banks[g] = []
            for b in range(GROUP // 2):
                bank = psum_t.tile([P, 2, 2, P], F32, name="bank")
                for i in range(2):
                    t = g * GROUP + 2 * b + i
                    words, idx = x_of_tile[t]
                    lo = idx * KW
                    for u in range(2):
                        if t in split:
                            source = split[t][:, u, :]
                        else:
                            source = words[:, lo + u : lo + KW : 2]
                        nc.tensor.transpose(bank[:, i, u, :], source, ident[:])
                banks[g].append(bank)

        def regroup(g):
            grp = work.tile([P, GROUP * P * 4], BF16, name="grp", align_bytes=64)
            gw = grp[:].bitcast(F32)
            for b, bank in enumerate(banks[g]):
                nc.vector.tensor_copy(
                    out=gw[:, 512 * b : 512 * (b + 1)].rearrange("p (i r u) -> p i r u", i=2, u=2),
                    in_=bank[:].rearrange("p i u r -> p i r u"),
                )
            grouped[g] = grp

        def quantise(g):
            codes = work.tile([P, GROUP * P], U32, name="codes", align_bytes=64)
            scales = work.tile([P, GROUP * P], U8, name="scales", align_bytes=64)
            nc.vector.quantize_mx(
                out=codes[:].bitcast(FP8X4), scales=scales[:], in_=grouped[g][:]
            )
            packed[g] = (codes, scales)

        def multiply(g):
            codes, scales = packed[g]
            for i in range(GROUP):
                t = g * GROUP + i
                cols = slice(i * P, (i + 1) * P)
                acc = psum_o.tile([P, OUT], F32, name="acc")
                for lo, hi in [(0, SPARSE), (SPARSE, OUT)]:
                    nc.tensor.matmul_mx(
                        out=acc[:, lo:hi],
                        lhsT=codes[:, cols].bitcast(FP8X4),
                        lhsT_scale=scales[:, cols],
                        rhs=w_codes[:, lo:hi].bitcast(FP8X4),
                        rhs_scale=w_scales[:, lo:hi],
                        start=True,
                        stop=True,
                    )
                o_sb, idx = out_of_tile[t]
                dst = o_sb[:, idx * OUT : (idx + 1) * OUT]
                if g >= GROUPS - SHARED_GROUPS and i % 2 == 1:
                    nc.vector.tensor_copy(out=dst, in_=acc[:])
                else:
                    nc.scalar.copy(out=dst, in_=acc[:])
                if t in store_after:
                    o_sb, first, n = store_after[t]
                    nc.sync.dma_start(
                        out=out_rows[:, first * OUT : (first + n) * OUT], in_=o_sb[:]
                    )

        for s in range(GROUPS + 2):
            if SPLIT_FROM <= s + 1 < GROUPS:
                split_words(s + 1)
            if s < GROUPS:
                transposes(s)
                regroup(s)
            if s == 0:
                quantise_weights()
            if 1 <= s <= GROUPS:
                quantise(s - 1)
            if s >= 2:
                multiply(s - 2)
